import numpy as np
import ml_dtypes


def mxq(x, axis, fmt="e4m3"):
    dtype, down = {"e4m3": (ml_dtypes.float8_e4m3fn, 7), "e5m2": (ml_dtypes.float8_e5m2, 14)}[fmt]
    v = np.moveaxis(np.asarray(x, np.float32).astype(ml_dtypes.bfloat16).astype(np.float64), axis, -1)
    blocks = v.reshape(v.shape[:-1] + (-1, 32))
    amax = np.abs(blocks).max(-1, keepdims=True)
    byte = np.maximum(np.where(amax > 0, np.frexp(amax)[1] - 1 + 127, 0) - down, 1)
    scale = np.exp2(byte - 127.0)
    codes = (blocks / scale).astype(np.float32).astype(dtype).astype(np.float64)
    return np.moveaxis((codes * scale).reshape(v.shape), -1, axis)


WIDE = False


def mx_kscale(k):
    if not WIDE:
        return np.ones(k)
    levels = np.array([10, -10, 5, -5, 0])
    if k % 512:
        return np.exp2(np.random.permutation(np.resize(levels, k // 32))).repeat(32)
    a = np.empty((k // 512, 16))
    for p in range(k // 512):
        a[p, :8] = np.random.permutation(np.resize(levels, 8))
        for g in range(8):
            far = levels[np.abs(levels - a[p, g]) >= 10]
            a[p, g + 8] = far[np.random.randint(len(far))]
    return np.exp2(a.ravel()).repeat(32)


BF16 = ml_dtypes.bfloat16


def bf(x):
    return np.asarray(x, np.float32).astype(BF16)


def f64(x):
    return np.asarray(x).astype(np.float64)


B, I, J, K, D = 4096, 256, 1024, 4, 2


def squash(x, axis=-1):
    norm = np.sqrt(np.sum(x * x, axis=axis, keepdims=True))
    scale = norm ** 2 / (1.0 + norm ** 2) / (norm + 1e-8)
    return scale * x


def setup_inputs():
    s = mx_kscale(J)
    c = 2.0 / np.sqrt(J * D * (K * K / 4.0 + K / 12.0))
    return {"X": bf(np.random.standard_normal((B, J, D)) * s[None, :, None]),
            "weight": bf(np.random.random((I, J, K, D)) * c / s[None, :, None, None])}


def reference(X, weight):
    xq = mxq(f64(X), 1, "e4m3")
    wq = mxq(f64(weight).sum(axis=2), 1, "e4m3")
    s = xq.transpose(2, 0, 1) @ wq.transpose(2, 1, 0)
    return squash(s.transpose(1, 2, 0), axis=-1)

@@ -1,0 +1,214 @@
+from contextlib import ExitStack
+
+import concourse.mybir as mybir
+from concourse.masks import make_identity
+
+F32 = mybir.dt.float32
+BF16 = mybir.dt.bfloat16
+U32 = mybir.dt.uint32
+U8 = mybir.dt.uint8
+FP8X4 = mybir.dt.float8_e4m3fn_x4
+ACT = mybir.ActivationFunctionType
+ALU = mybir.AluOpType
+
+B, I, J, K, D = 4096, 256, 1024, 4, 2
+P = 128
+FLOPS = 2 * B * I * J * D
+NT = B // P
+EPS = 1e-8
+TINY = 1e-30
+XBUFS = 8
+GP_UNITS = ()
+
+
+def tile_primary_capsule_t_kernel(tc, X, weight, out):
+    nc = tc.nc
+    Xz = X.rearrange("(n q) j d -> n q (j d)", q=P)
+    Wv = weight.rearrange("(t p) j k d -> t p (j k d)", p=P)
+    Ov = out.rearrange("(m e p) i d -> m p e (i d)", e=2, p=P)
+    with ExitStack() as ctx:
+        const = ctx.enter_context(tc.tile_pool(name="const", bufs=1))
+        xin = ctx.enter_context(tc.tile_pool(name="xin", bufs=XBUFS))
+        wtmp = ctx.enter_context(tc.tile_pool(name="wtmp", bufs=4))
+        grp = ctx.enter_context(tc.tile_pool(name="grp", bufs=3))
+        xqp = ctx.enter_context(tc.tile_pool(name="xqp", bufs=4))
+        ep = ctx.enter_context(tc.tile_pool(name="ep", bufs=4))
+        outp = ctx.enter_context(tc.tile_pool(name="outp", bufs=3))
+        tp = ctx.enter_context(tc.psum_pool(name="tp", bufs=4))
+        accp = ctx.enter_context(tc.psum_pool(name="accp", bufs=4))
+
+        warm = const.tile([P, 1], F32, name="warm")
+        nc.vector.memset(warm[:], 1.0)
+        nc.scalar.activation(out=warm[:], in_=warm[:], func=ACT.Abs_reciprocal_sqrt)
+        ident_b = const.tile([P, P], BF16, name="ident_b")
+        make_identity(nc, ident_b[:])
+        ident_f = const.tile([P, P], F32, name="ident_f")
+        make_identity(nc, ident_f[:])
+
+        x_t = {}
+        xt_t = {}
+        gx_t = {}
+        xq_t = {}
+        acc_t = {}
+        e_t = {}
+        o_t = {}
+        done = set()
+
+        def once(key):
+            if key in done:
+                return False
+            done.add(key)
+            return True
+
+        def load(n):
+            if 0 <= n < NT and once(("load", n)):
+                x_sb = xin.tile([P, J * D], BF16, name="x_sb")
+                nc.sync.dma_start(out=x_sb[:], in_=Xz[n])
+                x_t[n] = x_sb
+
+        def transposes(n):
+            if 0 <= n < NT and once(("T", n)):
+                banks = []
+                xv = x_t[n][:].rearrange("q (g p t d) -> q g p t d", g=2, p=P, d=D)
+                for d in range(D):
+                    xt = tp.tile([P, 2, 4, P], BF16, name="xt", tag="tp")
+                    for g in range(2):
+                        for t in range(4):
+                            nc.tensor.transpose(xt[:, g, t, :], xv[:, g, :, t, d], ident_b[:])
+                    banks.append(xt)
+                xt_t[n] = banks
+
+        def copy(n, d):
+            if 0 <= n < NT and once(("c", n, d)):
+                if d == 0:
+                    gx_new = grp.tile([P, D, 2, P, 4], BF16, name="gx", align_bytes=64)
+                    gx_t[n] = gx_new
+                nc.scalar.copy(out=gx_t[n][:, d], in_=xt_t[n][d][:].rearrange("p g t b -> p g b t"))
+
+        def quant(n):
+            if 0 <= n < NT and once(("Q", n)):
+                xq = xqp.tile([P, 4 * P], U32, name="xq", align_bytes=64)
+                xs = xqp.tile([P, 4 * P], U8, name="xs", align_bytes=64)
+                nc.vector.quantize_mx(out=xq[:].bitcast(FP8X4), scales=xs[:],
+                                      in_=gx_t[n][:].rearrange("p d g b s -> p (d g b s)"))
+                xq_t[n] = (xq, xs)
+
+        UNIT = 256 * K * D
+        w_raw = [const.tile([P, J * K * D], BF16, name="w_raw%d" % t) for t in range(2)]
+        units = [(g, t, hf) for g in range(2) for t in range(2) for hf in range(2)]
+        for (g, t, hf) in units:
+            e0 = (2 * g + hf) * UNIT
+            nc.sync.dma_start(out=w_raw[t][:, e0:e0 + UNIT], in_=Wv[t][:, e0:e0 + UNIT])
+        for n in range(XBUFS):
+            load(n)
+
+        gw = const.tile([P, 2, D, I, 4], BF16, name="gw", align_bytes=64)
+        wq = const.tile([P, 4 * I], U32, name="wq", align_bytes=64)
+        wsc = const.tile([P, 4 * I], U8, name="wsc", align_bytes=64)
+        parts = {}
+        for (g, t, hf) in units:
+            e0 = (2 * g + hf) * UNIT
+            w4 = w_raw[t][:, e0:e0 + UNIT].rearrange("p (j h c) -> p j h c", h=2, c=4)
+            if hf == 0:
+                part = wtmp.tile([P, 4, 512], F32, name="part")
+                parts[(g, t)] = part
+            nc.vector.tensor_tensor(out=parts[(g, t)][:, :, hf * 256:(hf + 1) * 256].rearrange("p c j -> p j c"),
+                                    in0=w4[:, :, 0, :], in1=w4[:, :, 1, :], op=ALU.add)
+        for g in range(2):
+            for t in range(2):
+                for d in range(D):
+                    wt = tp.tile([P, 4, P], F32, name="wt", tag="tp")
+                    for s in range(4):
+                        for e in range(2):
+                            nc.tensor.matmul(out=wt[:, s, :],
+                                             lhsT=parts[(g, t)][:, 2 * e + d, s:512:4],
+                                             rhs=ident_f[:], start=(e == 0), stop=(e == 1), is_transpose=True)
+                    nc.scalar.copy(out=gw[:, g, d, t * P:(t + 1) * P, :],
+                                   in_=wt[:].rearrange("p s i -> p i s"))
+            nc.vector.quantize_mx(out=wq[:, g * 2 * I:(g + 1) * 2 * I].bitcast(FP8X4),
+                                  scales=wsc[:, g * 2 * I:(g + 1) * 2 * I],
+                                  in_=gw[:, g].rearrange("p d i s -> p (d i s)"))
+
+        def mx(n):
+            if 0 <= n < NT:
+                xq, xs = xq_t[n]
+                acc = accp.tile([P, D, I], F32, name="acc")
+                for d in range(D):
+                    for g in range(2):
+                        cx = (2 * d + g) * P
+                        cw = (2 * g + d) * I
+                        nc.tensor.matmul_mx(out=acc[:, d, :],
+                                            lhsT=xq[:, cx:cx + P].bitcast(FP8X4),
+                                            lhsT_scale=xs[:, cx:cx + P],
+                                            rhs=wq[:, cw:cw + I].bitcast(FP8X4),
+                                            rhs_scale=wsc[:, cw:cw + I],
+                                            start=(g == 0), stop=(g == 1))
+                acc_t[n] = acc
+
+        def squares(n):
+            if 0 <= n < NT:
+                sq = ep.tile([P, D, I], F32, name="sq")
+                nc.scalar.activation(out=sq[:], in_=acc_t[n][:], func=ACT.Square)
+                e_t[n] = {"sq": sq}
+
+        def add_squares(n):
+            if 0 <= n < NT:
+                sq = e_t[n]["sq"]
+                n2 = ep.tile([P, I], F32, name="n2")
+                nc.vector.tensor_tensor(out=n2[:], in0=sq[:, 0, :], in1=sq[:, 1, :], op=ALU.add)
+                e_t[n]["n2"] = n2
+
+        def one_plus(n):
+            if 0 <= n < NT:
+                den = ep.tile([P, I], F32, name="den")
+                nc.vector.tensor_scalar_add(out=den[:], in0=e_t[n]["n2"][:], scalar1=1.0)
+                e_t[n]["den"] = den
+
+        def rnorm(n):
+            if 0 <= n < NT:
+                nn = ep.tile([P, I], F32, name="nn")
+                nc.scalar.activation(out=nn[:], in_=e_t[n]["n2"][:], func=ACT.Abs_reciprocal_sqrt,
+                                     bias=TINY, scale=1.0)
+                e_t[n]["nn"] = nn
+
+        def denom(n):
+            if 0 <= n < NT:
+                n2, nn, den = e_t[n]["n2"], e_t[n]["nn"], e_t[n]["den"]
+                nc.vector.tensor_tensor(out=nn[:], in0=n2[:], in1=nn[:], op=ALU.mult)
+                nc.vector.scalar_tensor_tensor(out=den[:], in0=nn[:], scalar=EPS, in1=den[:],
+                                               op0=ALU.add, op1=ALU.mult)
+
+        def factor(n):
+            if 0 <= n < NT:
+                rr = ep.tile([P, I], F32, name="rr")
+                nc.scalar.activation(out=rr[:], in_=e_t[n]["den"][:], func=ACT.Abs_reciprocal_sqrt)
+                nc.scalar.activation(out=rr[:], in_=rr[:], func=ACT.Square)
+                e_t[n]["rr"] = rr
+
+        def final(n):
+            if 0 <= n < NT:
+                m, e = divmod(n, 2)
+                rr = e_t[n]["rr"]
+                nc.vector.tensor_tensor(out=rr[:], in0=e_t[n]["n2"][:], in1=rr[:], op=ALU.mult)
+                if e == 0:
+                    o_new = outp.tile([P, 2, I, D], F32, name="o_sb")
+                    o_t[m] = o_new
+                nc.vector.tensor_tensor(out=o_t[m][:, e], in0=acc_t[n][:].rearrange("p d i -> p i d"),
+                                        in1=e_t[n]["rr"][:].unsqueeze(2).to_broadcast([P, I, D]), op=ALU.mult)
+                if e == 1:
+                    nc.sync.dma_start(out=Ov[m], in_=o_t[m][:].rearrange("p e i d -> p e (i d)"))
+
+        for i in range(-4, NT + 2):
+            squares(i)
+            factor(i - 2)
+            quant(i + 2)
+            copy(i + 3, 0)
+            copy(i + 3, 1)
+            load(i + 4 + XBUFS - 2)
+            add_squares(i)
+            denom(i - 1)
+            mx(i + 1)
+            transposes(i + 4)
+            rnorm(i)
+            final(i - 2)
+            one_plus(i)

@@ -69,21 +69,22 @@ def tile_primary_capsule_t_kernel(tc, X, weight, out):
         def transposes(n):
             if 0 <= n < NT and once(("T", n)):
                 banks = []
-                xv = x_t[n][:].rearrange("q (g p t d) -> q g p t d", g=2, p=P, d=D)
-                for d in range(D):
-                    xt = tp.tile([P, 2, 4, P], BF16, name="xt", tag="tp")
-                    for g in range(2):
-                        for t in range(4):
-                            nc.tensor.transpose(xt[:, g, t, :], xv[:, g, :, t, d], ident_b[:])
+                words = x_t[n][:].bitcast(F32)
+                for g in range(2):
+                    xt = tp.tile([P, 4, P], F32, name="xt", tag="tp")
+                    for t in range(4):
+                        nc.tensor.transpose(xt[:, t, :], words[:, 512 * g + t:512 * (g + 1):4], ident_f[:])
                     banks.append(xt)
                 xt_t[n] = banks
 
-        def copy(n, d):
-            if 0 <= n < NT and once(("c", n, d)):
-                if d == 0:
+        def copy(n, g):
+            if 0 <= n < NT and once(("c", n, g)):
+                if g == 0:
                     gx_new = grp.tile([P, D, 2, P, 4], BF16, name="gx", align_bytes=64)
                     gx_t[n] = gx_new
-                nc.scalar.copy(out=gx_t[n][:, d], in_=xt_t[n][d][:].rearrange("p g t b -> p g b t"))
+                nc.scalar.copy(out=gx_t[n][:, :, g],
+                               in_=xt_t[n][g][:].rearrange("p t b -> p (t b)").bitcast(BF16).rearrange(
+                                   "p (t b d) -> p d b t", t=4, d=D))
 
         def quant(n):
             if 0 <= n < NT and once(("Q", n)):

@@ -16,9 +16,9 @@ P = 128
 FLOPS = 2 * B * I * J * D
 NT = B // P
 EPS = 1e-8
-TINY = 1e-30
+TINY = 1e-26
 XBUFS = 8
-GP_UNITS = ()
+AHEAD = 7
 
 
 def tile_primary_capsule_t_kernel(tc, X, weight, out):
@@ -31,7 +31,7 @@ def tile_primary_capsule_t_kernel(tc, X, weight, out):
         xin = ctx.enter_context(tc.tile_pool(name="xin", bufs=XBUFS))
         wtmp = ctx.enter_context(tc.tile_pool(name="wtmp", bufs=4))
         grp = ctx.enter_context(tc.tile_pool(name="grp", bufs=3))
-        xqp = ctx.enter_context(tc.tile_pool(name="xqp", bufs=4))
+        xqp = ctx.enter_context(tc.tile_pool(name="xqp", bufs=12))
         ep = ctx.enter_context(tc.tile_pool(name="ep", bufs=4))
         outp = ctx.enter_context(tc.tile_pool(name="outp", bufs=3))
         tp = ctx.enter_context(tc.psum_pool(name="tp", bufs=4))
@@ -40,8 +40,6 @@ def tile_primary_capsule_t_kernel(tc, X, weight, out):
         warm = const.tile([P, 1], F32, name="warm")
         nc.vector.memset(warm[:], 1.0)
         nc.scalar.activation(out=warm[:], in_=warm[:], func=ACT.Abs_reciprocal_sqrt)
-        ident_b = const.tile([P, P], BF16, name="ident_b")
-        make_identity(nc, ident_b[:])
         ident_f = const.tile([P, P], F32, name="ident_f")
         make_identity(nc, ident_f[:])
 
@@ -77,14 +75,18 @@ def tile_primary_capsule_t_kernel(tc, X, weight, out):
                     banks.append(xt)
                 xt_t[n] = banks
 
-        def copy(n, g):
-            if 0 <= n < NT and once(("c", n, g)):
-                if g == 0:
-                    gx_new = grp.tile([P, D, 2, P, 4], BF16, name="gx", align_bytes=64)
-                    gx_t[n] = gx_new
-                nc.scalar.copy(out=gx_t[n][:, :, g],
-                               in_=xt_t[n][g][:].rearrange("p t b -> p (t b)").bitcast(BF16).rearrange(
-                                   "p (t b d) -> p d b t", t=4, d=D))
+        def copy(n):
+            if 0 <= n < NT and once(("c", n)):
+                gx = grp.tile([P, D, 2, P, 4], BF16, name="gx", align_bytes=64)
+                gx_t[n] = gx
+                for h in range(2):
+                    dst = gx[:, :, h]
+                    src = xt_t[n][h][:].rearrange("p t b -> p (t b)").bitcast(BF16).rearrange(
+                        "p (t b d) -> p d b t", t=4, d=D)
+                    if h == 0:
+                        nc.scalar.copy(out=dst, in_=src)
+                    else:
+                        nc.vector.tensor_copy(out=dst, in_=src)
 
         def quant(n):
             if 0 <= n < NT and once(("Q", n)):
@@ -94,41 +96,54 @@ def tile_primary_capsule_t_kernel(tc, X, weight, out):
                                       in_=gx_t[n][:].rearrange("p d g b s -> p (d g b s)"))
                 xq_t[n] = (xq, xs)
 
-        UNIT = 256 * K * D
+        GROUP = 512 * K * D
         w_raw = [const.tile([P, J * K * D], BF16, name="w_raw%d" % t) for t in range(2)]
-        units = [(g, t, hf) for g in range(2) for t in range(2) for hf in range(2)]
-        for (g, t, hf) in units:
-            e0 = (2 * g + hf) * UNIT
-            nc.sync.dma_start(out=w_raw[t][:, e0:e0 + UNIT], in_=Wv[t][:, e0:e0 + UNIT])
-        for n in range(XBUFS):
-            load(n)
+        groups = [(0, 0), (0, 1), (1, 0), (1, 1)]
+        for m, (g, t) in enumerate(groups):
+            load(2 * m)
+            load(2 * m + 1)
+            nc.sync.dma_start(out=w_raw[t][:, g * GROUP:(g + 1) * GROUP], in_=Wv[t][:, g * GROUP:(g + 1) * GROUP])
+
+        def prepare(n):
+            transposes(n)
+            copy(n)
+            quant(n)
 
         gw = const.tile([P, 2, D, I, 4], BF16, name="gw", align_bytes=64)
         wq = const.tile([P, 4 * I], U32, name="wq", align_bytes=64)
         wsc = const.tile([P, 4 * I], U8, name="wsc", align_bytes=64)
-        parts = {}
-        for (g, t, hf) in units:
-            e0 = (2 * g + hf) * UNIT
-            w4 = w_raw[t][:, e0:e0 + UNIT].rearrange("p (j h c) -> p j h c", h=2, c=4)
-            if hf == 0:
-                part = wtmp.tile([P, 4, 512], F32, name="part")
-                parts[(g, t)] = part
-            nc.vector.tensor_tensor(out=parts[(g, t)][:, :, hf * 256:(hf + 1) * 256].rearrange("p c j -> p j c"),
-                                    in0=w4[:, :, 0, :], in1=w4[:, :, 1, :], op=ALU.add)
-        for g in range(2):
-            for t in range(2):
-                for d in range(D):
-                    wt = tp.tile([P, 4, P], F32, name="wt", tag="tp")
-                    for s in range(4):
-                        for e in range(2):
-                            nc.tensor.matmul(out=wt[:, s, :],
-                                             lhsT=parts[(g, t)][:, 2 * e + d, s:512:4],
-                                             rhs=ident_f[:], start=(e == 0), stop=(e == 1), is_transpose=True)
-                    nc.scalar.copy(out=gw[:, g, d, t * P:(t + 1) * P, :],
-                                   in_=wt[:].rearrange("p s i -> p i s"))
+
+        def weight_group(g, t):
+            part = wtmp.tile([P, P, 4, 2, D], F32, name="part")
+            w2 = w_raw[t][:, g * GROUP:(g + 1) * GROUP].rearrange("i (j e c) -> i j e c", e=2, c=4)
+            for h in range(2):
+                nc.vector.tensor_tensor(out=part[:, 64 * h:64 * (h + 1)].rearrange("i p s e d -> i (p s) (e d)"),
+                                        in0=w2[:, 256 * h:256 * (h + 1), 0, :],
+                                        in1=w2[:, 256 * h:256 * (h + 1), 1, :], op=ALU.add)
+            for d in range(D):
+                wt = tp.tile([P, 4, P], F32, name="wt", tag="tp")
+                for s in range(4):
+                    for e in range(2):
+                        nc.tensor.matmul(out=wt[:, s, :], lhsT=part[:, :, s, e, d], rhs=ident_f[:],
+                                         start=(e == 0), stop=(e == 1), is_transpose=True)
+                dst = gw[:, g, d, t * P:(t + 1) * P, :]
+                src = wt[:].rearrange("p s i -> p i s")
+                if d == 0:
+                    nc.scalar.copy(out=dst, in_=src)
+                else:
+                    nc.vector.tensor_copy(out=dst, in_=src)
+
+        def weight_quant(g):
             nc.vector.quantize_mx(out=wq[:, g * 2 * I:(g + 1) * 2 * I].bitcast(FP8X4),
                                   scales=wsc[:, g * 2 * I:(g + 1) * 2 * I],
                                   in_=gw[:, g].rearrange("p d i s -> p (d i s)"))
+
+        for m, (g, t) in enumerate(groups):
+            prepare(2 * m)
+            prepare(2 * m + 1)
+            weight_group(g, t)
+            if t == 1:
+                weight_quant(g)
 
         def mx(n):
             if 0 <= n < NT:
@@ -156,60 +171,56 @@ def tile_primary_capsule_t_kernel(tc, X, weight, out):
             if 0 <= n < NT:
                 sq = e_t[n]["sq"]
                 n2 = ep.tile([P, I], F32, name="n2")
-                nc.vector.tensor_tensor(out=n2[:], in0=sq[:, 0, :], in1=sq[:, 1, :], op=ALU.add)
+                nc.gpsimd.tensor_tensor(out=n2[:], in0=sq[:, 0, :], in1=sq[:, 1, :], op=ALU.add)
                 e_t[n]["n2"] = n2
-
-        def one_plus(n):
-            if 0 <= n < NT:
-                den = ep.tile([P, I], F32, name="den")
-                nc.vector.tensor_scalar_add(out=den[:], in0=e_t[n]["n2"][:], scalar1=1.0)
-                e_t[n]["den"] = den
 
         def rnorm(n):
             if 0 <= n < NT:
-                nn = ep.tile([P, I], F32, name="nn")
-                nc.scalar.activation(out=nn[:], in_=e_t[n]["n2"][:], func=ACT.Abs_reciprocal_sqrt,
+                r = ep.tile([P, I], F32, name="r")
+                nc.scalar.activation(out=r[:], in_=e_t[n]["n2"][:], func=ACT.Abs_reciprocal_sqrt,
                                      bias=TINY, scale=1.0)
-                e_t[n]["nn"] = nn
+                c1 = ep.tile([P, I], F32, name="c1")
+                nc.gpsimd.tensor_scalar(out=c1[:], in0=r[:], scalar1=EPS, scalar2=1.0, op0=ALU.mult, op1=ALU.add)
+                e_t[n]["r"] = r
+                e_t[n]["c1"] = c1
 
-        def denom(n):
+        def inverse(n):
             if 0 <= n < NT:
-                n2, nn, den = e_t[n]["n2"], e_t[n]["nn"], e_t[n]["den"]
-                nc.vector.tensor_tensor(out=nn[:], in0=n2[:], in1=nn[:], op=ALU.mult)
-                nc.vector.scalar_tensor_tensor(out=den[:], in0=nn[:], scalar=EPS, in1=den[:],
+                r = e_t[n]["r"]
+                w = ep.tile([P, I], F32, name="w")
+                nc.vector.scalar_tensor_tensor(out=w[:], in0=e_t[n]["n2"][:], scalar=1.0, in1=r[:],
                                                op0=ALU.add, op1=ALU.mult)
+                p = ep.tile([P, I], F32, name="p")
+                nc.gpsimd.tensor_tensor(out=p[:], in0=w[:], in1=e_t[n]["c1"][:], op=ALU.mult)
+                e_t[n]["w"] = p
 
         def factor(n):
             if 0 <= n < NT:
-                rr = ep.tile([P, I], F32, name="rr")
-                nc.scalar.activation(out=rr[:], in_=e_t[n]["den"][:], func=ACT.Abs_reciprocal_sqrt)
-                nc.scalar.activation(out=rr[:], in_=rr[:], func=ACT.Square)
-                e_t[n]["rr"] = rr
+                f = ep.tile([P, I], F32, name="f")
+                nc.scalar.activation(out=f[:], in_=e_t[n]["w"][:], func=ACT.Square)
+                nc.scalar.activation(out=f[:], in_=f[:], func=ACT.Abs_reciprocal_sqrt)
+                e_t[n]["f"] = f
 
         def final(n):
             if 0 <= n < NT:
                 m, e = divmod(n, 2)
-                rr = e_t[n]["rr"]
-                nc.vector.tensor_tensor(out=rr[:], in0=e_t[n]["n2"][:], in1=rr[:], op=ALU.mult)
                 if e == 0:
                     o_new = outp.tile([P, 2, I, D], F32, name="o_sb")
                     o_t[m] = o_new
                 nc.vector.tensor_tensor(out=o_t[m][:, e], in0=acc_t[n][:].rearrange("p d i -> p i d"),
-                                        in1=e_t[n]["rr"][:].unsqueeze(2).to_broadcast([P, I, D]), op=ALU.mult)
+                                        in1=e_t[n]["f"][:].unsqueeze(2).to_broadcast([P, I, D]), op=ALU.mult)
                 if e == 1:
                     nc.sync.dma_start(out=Ov[m], in_=o_t[m][:].rearrange("p e i d -> p e (i d)"))
 
-        for i in range(-4, NT + 2):
+        for i in range(-1, NT + 2):
             squares(i)
             factor(i - 2)
-            quant(i + 2)
-            copy(i + 3, 0)
-            copy(i + 3, 1)
-            load(i + 4 + XBUFS - 2)
+            quant(i + AHEAD)
+            copy(i + AHEAD + 1)
+            load(i + XBUFS + 1)
             add_squares(i)
-            denom(i - 1)
+            inverse(i - 1)
             mx(i + 1)
-            transposes(i + 4)
+            transposes(i + AHEAD + 2)
             rnorm(i)
             final(i - 2)
-            one_plus(i)

@@ -18,7 +18,7 @@ NT = B // P
 EPS = 1e-8
 TINY = 1e-26
 XBUFS = 8
-AHEAD = 7
+HEAD = 20
 
 
 def tile_primary_capsule_t_kernel(tc, X, weight, out):
@@ -31,11 +31,11 @@ def tile_primary_capsule_t_kernel(tc, X, weight, out):
         xin = ctx.enter_context(tc.tile_pool(name="xin", bufs=XBUFS))
         wtmp = ctx.enter_context(tc.tile_pool(name="wtmp", bufs=4))
         grp = ctx.enter_context(tc.tile_pool(name="grp", bufs=3))
-        xqp = ctx.enter_context(tc.tile_pool(name="xqp", bufs=12))
+        xqp = ctx.enter_context(tc.tile_pool(name="xqp", bufs=23))
         ep = ctx.enter_context(tc.tile_pool(name="ep", bufs=4))
         outp = ctx.enter_context(tc.tile_pool(name="outp", bufs=3))
-        tp = ctx.enter_context(tc.psum_pool(name="tp", bufs=4))
-        accp = ctx.enter_context(tc.psum_pool(name="accp", bufs=4))
+        tp = ctx.enter_context(tc.psum_pool(name="tp", bufs=3))
+        accp = ctx.enter_context(tc.psum_pool(name="accp", bufs=5))
 
         warm = const.tile([P, 1], F32, name="warm")
         nc.vector.memset(warm[:], 1.0)
@@ -75,18 +75,18 @@ def tile_primary_capsule_t_kernel(tc, X, weight, out):
                     banks.append(xt)
                 xt_t[n] = banks
 
-        def copy(n):
-            if 0 <= n < NT and once(("c", n)):
-                gx = grp.tile([P, D, 2, P, 4], BF16, name="gx", align_bytes=64)
-                gx_t[n] = gx
-                for h in range(2):
-                    dst = gx[:, :, h]
-                    src = xt_t[n][h][:].rearrange("p t b -> p (t b)").bitcast(BF16).rearrange(
-                        "p (t b d) -> p d b t", t=4, d=D)
-                    if h == 0:
-                        nc.scalar.copy(out=dst, in_=src)
-                    else:
-                        nc.vector.tensor_copy(out=dst, in_=src)
+        def copy(n, g):
+            if 0 <= n < NT and once(("c", n, g)):
+                if g == 0:
+                    gx_new = grp.tile([P, D, 2, P, 4], BF16, name="gx", align_bytes=64)
+                    gx_t[n] = gx_new
+                dst = gx_t[n][:, :, g]
+                src = xt_t[n][g][:].rearrange("p t b -> p (t b)").bitcast(BF16).rearrange(
+                    "p (t b d) -> p d b t", t=4, d=D)
+                if g == 0 or n % 4 == 0:
+                    nc.scalar.copy(out=dst, in_=src)
+                else:
+                    nc.vector.tensor_copy(out=dst, in_=src)
 
         def quant(n):
             if 0 <= n < NT and once(("Q", n)):
@@ -96,59 +96,54 @@ def tile_primary_capsule_t_kernel(tc, X, weight, out):
                                       in_=gx_t[n][:].rearrange("p d g b s -> p (d g b s)"))
                 xq_t[n] = (xq, xs)
 
-        GROUP = 512 * K * D
+        UNIT = 256 * K * D
         w_raw = [const.tile([P, J * K * D], BF16, name="w_raw%d" % t) for t in range(2)]
-        groups = [(0, 0), (0, 1), (1, 0), (1, 1)]
-        for m, (g, t) in enumerate(groups):
-            load(2 * m)
-            load(2 * m + 1)
-            nc.sync.dma_start(out=w_raw[t][:, g * GROUP:(g + 1) * GROUP], in_=Wv[t][:, g * GROUP:(g + 1) * GROUP])
-
-        def prepare(n):
-            transposes(n)
-            copy(n)
-            quant(n)
-
         gw = const.tile([P, 2, D, I, 4], BF16, name="gw", align_bytes=64)
         wq = const.tile([P, 4 * I], U32, name="wq", align_bytes=64)
         wsc = const.tile([P, 4 * I], U8, name="wsc", align_bytes=64)
+        parts = {}
 
-        def weight_group(g, t):
-            part = wtmp.tile([P, P, 4, 2, D], F32, name="part")
-            w2 = w_raw[t][:, g * GROUP:(g + 1) * GROUP].rearrange("i (j e c) -> i j e c", e=2, c=4)
-            for h in range(2):
-                nc.vector.tensor_tensor(out=part[:, 64 * h:64 * (h + 1)].rearrange("i p s e d -> i (p s) (e d)"),
-                                        in0=w2[:, 256 * h:256 * (h + 1), 0, :],
-                                        in1=w2[:, 256 * h:256 * (h + 1), 1, :], op=ALU.add)
-            for d in range(D):
-                wt = tp.tile([P, 4, P], F32, name="wt", tag="tp")
-                for s in range(4):
-                    for e in range(2):
-                        nc.tensor.matmul(out=wt[:, s, :], lhsT=part[:, :, s, e, d], rhs=ident_f[:],
-                                         start=(e == 0), stop=(e == 1), is_transpose=True)
-                dst = gw[:, g, d, t * P:(t + 1) * P, :]
-                src = wt[:].rearrange("p s i -> p i s")
-                if d == 0:
-                    nc.scalar.copy(out=dst, in_=src)
-                else:
-                    nc.vector.tensor_copy(out=dst, in_=src)
+        def weight_load(g, t, h):
+            e0 = (2 * g + h) * UNIT
+            nc.sync.dma_start(out=w_raw[t][:, e0:e0 + UNIT], in_=Wv[t][:, e0:e0 + UNIT])
+
+        def weight_add(g, t, h):
+            e0 = (2 * g + h) * UNIT
+            w2 = w_raw[t][:, e0:e0 + UNIT].rearrange("i (j e c) -> i j e c", e=2, c=4)
+            if h == 0:
+                part = wtmp.tile([P, P, 4, 2, D], F32, name="part")
+                parts[(g, t)] = part
+            nc.gpsimd.tensor_tensor(out=parts[(g, t)][:, 64 * h:64 * (h + 1)].rearrange("i p s e d -> i (p s) (e d)"),
+                                 in0=w2[:, :, 0, :], in1=w2[:, :, 1, :],
+                                    op=ALU.add)
+
+        wt_t = {}
+
+        def weight_transposes(g, t, d):
+            wt = accp.tile([P, 4, P], F32, name="wt", tag="acc")
+            wt_t[(g, t, d)] = wt
+            for s in range(4):
+                for e in range(2):
+                    nc.tensor.matmul(out=wt[:, s, :], lhsT=parts[(g, t)][:, :, s, e, d], rhs=ident_f[:],
+                                     start=(e == 0), stop=(e == 1), is_transpose=True)
+
+        def weight_copy(g, t, d):
+            dst = gw[:, g, d, t * P:(t + 1) * P, :]
+            src = wt_t[(g, t, d)][:].rearrange("p s i -> p i s")
+            if d == 0:
+                nc.scalar.copy(out=dst, in_=src)
+            else:
+                nc.vector.tensor_copy(out=dst, in_=src)
 
         def weight_quant(g):
             nc.vector.quantize_mx(out=wq[:, g * 2 * I:(g + 1) * 2 * I].bitcast(FP8X4),
                                   scales=wsc[:, g * 2 * I:(g + 1) * 2 * I],
                                   in_=gw[:, g].rearrange("p d i s -> p (d i s)"))
 
-        for m, (g, t) in enumerate(groups):
-            prepare(2 * m)
-            prepare(2 * m + 1)
-            weight_group(g, t)
-            if t == 1:
-                weight_quant(g)
-
         def mx(n):
             if 0 <= n < NT:
                 xq, xs = xq_t[n]
-                acc = accp.tile([P, D, I], F32, name="acc")
+                acc = accp.tile([P, D, I], F32, name="acc", tag="acc")
                 for d in range(D):
                     for g in range(2):
                         cx = (2 * d + g) * P
@@ -171,7 +166,7 @@ def tile_primary_capsule_t_kernel(tc, X, weight, out):
             if 0 <= n < NT:
                 sq = e_t[n]["sq"]
                 n2 = ep.tile([P, I], F32, name="n2")
-                nc.gpsimd.tensor_tensor(out=n2[:], in0=sq[:, 0, :], in1=sq[:, 1, :], op=ALU.add)
+                nc.vector.tensor_tensor(out=n2[:], in0=sq[:, 0, :], in1=sq[:, 1, :], op=ALU.add)
                 e_t[n]["n2"] = n2
 
         def rnorm(n):
@@ -179,25 +174,22 @@ def tile_primary_capsule_t_kernel(tc, X, weight, out):
                 r = ep.tile([P, I], F32, name="r")
                 nc.scalar.activation(out=r[:], in_=e_t[n]["n2"][:], func=ACT.Abs_reciprocal_sqrt,
                                      bias=TINY, scale=1.0)
-                c1 = ep.tile([P, I], F32, name="c1")
-                nc.gpsimd.tensor_scalar(out=c1[:], in0=r[:], scalar1=EPS, scalar2=1.0, op0=ALU.mult, op1=ALU.add)
                 e_t[n]["r"] = r
-                e_t[n]["c1"] = c1
 
         def inverse(n):
             if 0 <= n < NT:
                 r = e_t[n]["r"]
                 w = ep.tile([P, I], F32, name="w")
-                nc.vector.scalar_tensor_tensor(out=w[:], in0=e_t[n]["n2"][:], scalar=1.0, in1=r[:],
+                nc.vector.scalar_tensor_tensor(out=w[:], in0=r[:], scalar=1.0 / EPS, in1=r[:],
                                                op0=ALU.add, op1=ALU.mult)
-                p = ep.tile([P, I], F32, name="p")
-                nc.gpsimd.tensor_tensor(out=p[:], in0=w[:], in1=e_t[n]["c1"][:], op=ALU.mult)
-                e_t[n]["w"] = p
+                nc.vector.scalar_tensor_tensor(out=w[:], in0=e_t[n]["n2"][:], scalar=1.0, in1=w[:],
+                                               op0=ALU.add, op1=ALU.mult)
+                e_t[n]["w"] = w
 
         def factor(n):
             if 0 <= n < NT:
                 f = ep.tile([P, I], F32, name="f")
-                nc.scalar.activation(out=f[:], in_=e_t[n]["w"][:], func=ACT.Square)
+                nc.scalar.activation(out=f[:], in_=e_t[n]["w"][:], func=ACT.Square, scale=EPS)
                 nc.scalar.activation(out=f[:], in_=f[:], func=ACT.Abs_reciprocal_sqrt)
                 e_t[n]["f"] = f
 
@@ -212,15 +204,51 @@ def tile_primary_capsule_t_kernel(tc, X, weight, out):
                 if e == 1:
                     nc.sync.dma_start(out=Ov[m], in_=o_t[m][:].rearrange("p e i d -> p e (i d)"))
 
-        for i in range(-1, NT + 2):
-            squares(i)
-            factor(i - 2)
-            quant(i + AHEAD)
-            copy(i + AHEAD + 1)
-            load(i + XBUFS + 1)
-            add_squares(i)
-            inverse(i - 1)
-            mx(i + 1)
-            transposes(i + AHEAD + 2)
-            rnorm(i)
-            final(i - 2)
+        order = [(g, t) for g in range(2) for t in range(2)]
+        loads = []
+        for u in range(8):
+            loads += [(load, (2 * u,)), (load, (2 * u + 1,)), (weight_load, order[u // 2] + (u % 2,))]
+        loads += [(load, (n,)) for n in range(16, HEAD + XBUFS)]
+        done_loads = [0]
+
+        def issue_loads(n):
+            while done_loads[0] < len(loads):
+                what, args = loads[done_loads[0]]
+                if what is load and args[0] > n + XBUFS - 1:
+                    break
+                what(*args)
+                if what is weight_load:
+                    weight_add(*args)
+                done_loads[0] += 1
+
+        with tc.manual_schedule(engines={mybir.EngineType.PE, mybir.EngineType.Activation, mybir.EngineType.DVE}):
+            issue_loads(0)
+            transposes(0)
+            for n in range(HEAD):
+                m, d = divmod(n - 6, 4)
+                weights_now = 0 <= m < 4 and d < D
+                if weights_now:
+                    weight_transposes(*order[m], d)
+                transposes(n + 1)
+                copy(n, 0)
+                copy(n, 1)
+                if weights_now:
+                    weight_copy(*order[m], d)
+                    if d == 1 and m % 2 == 1:
+                        weight_quant(m // 2)
+                quant(n - 1)
+                issue_loads(n + 1)
+            for i in range(-1, NT + 4):
+                ready = HEAD + (i + 1) * (NT + 2 - HEAD) // (NT - 1)
+                transposes(ready + 1)
+                mx(i + 1)
+                rnorm(i - 2)
+                inverse(i - 2)
+                factor(i - 3)
+                add_squares(i - 1)
+                final(i - 3)
+                load(ready + XBUFS - 1)
+                quant(ready - 1)
+                copy(ready, 0)
+                copy(ready, 1)
+                squares(i)

@@ -18,7 +18,7 @@ NT = B // P
 EPS = 1e-8
 TINY = 1e-26
 XBUFS = 8
-HEAD = 20
+HEAD = 22
 
 
 def tile_primary_capsule_t_kernel(tc, X, weight, out):
@@ -31,11 +31,10 @@ def tile_primary_capsule_t_kernel(tc, X, weight, out):
         xin = ctx.enter_context(tc.tile_pool(name="xin", bufs=XBUFS))
         wtmp = ctx.enter_context(tc.tile_pool(name="wtmp", bufs=4))
         grp = ctx.enter_context(tc.tile_pool(name="grp", bufs=3))
-        xqp = ctx.enter_context(tc.tile_pool(name="xqp", bufs=23))
+        xqp = ctx.enter_context(tc.tile_pool(name="xqp", bufs=25))
         ep = ctx.enter_context(tc.tile_pool(name="ep", bufs=4))
         outp = ctx.enter_context(tc.tile_pool(name="outp", bufs=3))
-        tp = ctx.enter_context(tc.psum_pool(name="tp", bufs=3))
-        accp = ctx.enter_context(tc.psum_pool(name="accp", bufs=5))
+        banks = ctx.enter_context(tc.psum_pool(name="banks", bufs=8))
 
         warm = const.tile([P, 1], F32, name="warm")
         nc.vector.memset(warm[:], 1.0)
@@ -66,14 +65,14 @@ def tile_primary_capsule_t_kernel(tc, X, weight, out):
 
         def transposes(n):
             if 0 <= n < NT and once(("T", n)):
-                banks = []
+                xts = []
                 words = x_t[n][:].bitcast(F32)
                 for g in range(2):
-                    xt = tp.tile([P, 4, P], F32, name="xt", tag="tp")
+                    xt = banks.tile([P, 4, P], F32, name="xt", tag="bank")
                     for t in range(4):
                         nc.tensor.transpose(xt[:, t, :], words[:, 512 * g + t:512 * (g + 1):4], ident_f[:])
-                    banks.append(xt)
-                xt_t[n] = banks
+                    xts.append(xt)
+                xt_t[n] = xts
 
         def copy(n, g):
             if 0 <= n < NT and once(("c", n, g)):
@@ -120,7 +119,7 @@ def tile_primary_capsule_t_kernel(tc, X, weight, out):
         wt_t = {}
 
         def weight_transposes(g, t, d):
-            wt = accp.tile([P, 4, P], F32, name="wt", tag="acc")
+            wt = banks.tile([P, 4, P], F32, name="wt", tag="bank")
             wt_t[(g, t, d)] = wt
             for s in range(4):
                 for e in range(2):
@@ -143,7 +142,7 @@ def tile_primary_capsule_t_kernel(tc, X, weight, out):
         def mx(n):
             if 0 <= n < NT:
                 xq, xs = xq_t[n]
-                acc = accp.tile([P, D, I], F32, name="acc", tag="acc")
+                acc = banks.tile([P, D, I], F32, name="acc", tag="bank")
                 for d in range(D):
                     for g in range(2):
                         cx = (2 * d + g) * P
@@ -221,11 +220,11 @@ def tile_primary_capsule_t_kernel(tc, X, weight, out):
                     weight_add(*args)
                 done_loads[0] += 1
 
-        with tc.manual_schedule(engines={mybir.EngineType.PE, mybir.EngineType.Activation, mybir.EngineType.DVE}):
+        with tc.manual_schedule(engines={mybir.EngineType.PE}):
             issue_loads(0)
             transposes(0)
             for n in range(HEAD):
-                m, d = divmod(n - 6, 4)
+                m, d = divmod(n - 8, 4)
                 weights_now = 0 <= m < 4 and d < D
                 if weights_now:
                     weight_transposes(*order[m], d)

@@ -108,13 +108,13 @@ def tile_primary_capsule_t_kernel(tc, X, weight, out):
 
         def weight_add(g, t, h):
             e0 = (2 * g + h) * UNIT
-            w2 = w_raw[t][:, e0:e0 + UNIT].rearrange("i (j e c) -> i j e c", e=2, c=4)
+            w2 = w_raw[t][:, e0:e0 + UNIT].rearrange("i (p s a e d) -> i a e s p d", s=4, a=2, e=2, d=D)
             if h == 0:
-                part = wtmp.tile([P, P, 4, 2, D], F32, name="part")
+                part = wtmp.tile([P, 2, 4, P, D], F32, name="part")
                 parts[(g, t)] = part
-            nc.gpsimd.tensor_tensor(out=parts[(g, t)][:, 64 * h:64 * (h + 1)].rearrange("i p s e d -> i (p s) (e d)"),
-                                 in0=w2[:, :, 0, :], in1=w2[:, :, 1, :],
-                                    op=ALU.add)
+            for e in range(2):
+                nc.gpsimd.tensor_tensor(out=parts[(g, t)][:, e, :, 64 * h:64 * (h + 1), :],
+                                        in0=w2[:, 0, e], in1=w2[:, 1, e], op=ALU.add)
 
         wt_t = {}
 
@@ -123,7 +123,7 @@ def tile_primary_capsule_t_kernel(tc, X, weight, out):
             wt_t[(g, t, d)] = wt
             for s in range(4):
                 for e in range(2):
-                    nc.tensor.matmul(out=wt[:, s, :], lhsT=parts[(g, t)][:, :, s, e, d], rhs=ident_f[:],
+                    nc.tensor.matmul(out=wt[:, s, :], lhsT=parts[(g, t)][:, e, s, :, d], rhs=ident_f[:],
                                      start=(e == 0), stop=(e == 1), is_transpose=True)
 
         def weight_copy(g, t, d):

@@ -18,6 +18,7 @@ NT = B // P
 EPS = 1e-8
 TINY = 1e-26
 XBUFS = 8
+SUMMED = (0, 1)
 HEAD = 22
 
 
@@ -39,6 +40,8 @@ def tile_primary_capsule_t_kernel(tc, X, weight, out):
         warm = const.tile([P, 1], F32, name="warm")
         nc.vector.memset(warm[:], 1.0)
         nc.scalar.activation(out=warm[:], in_=warm[:], func=ACT.Abs_reciprocal_sqrt)
+        ident_b = const.tile([P, P], BF16, name="ident_b")
+        make_identity(nc, ident_b[:])
         ident_f = const.tile([P, P], F32, name="ident_f")
         make_identity(nc, ident_f[:])
 
@@ -107,13 +110,15 @@ def tile_primary_capsule_t_kernel(tc, X, weight, out):
             nc.sync.dma_start(out=w_raw[t][:, e0:e0 + UNIT], in_=Wv[t][:, e0:e0 + UNIT])
 
         def weight_add(g, t, h):
+            if (g, t) != SUMMED:
+                return
             e0 = (2 * g + h) * UNIT
             w2 = w_raw[t][:, e0:e0 + UNIT].rearrange("i (p s a e d) -> i a e s p d", s=4, a=2, e=2, d=D)
             if h == 0:
                 part = wtmp.tile([P, 2, 4, P, D], F32, name="part")
                 parts[(g, t)] = part
             for e in range(2):
-                nc.gpsimd.tensor_tensor(out=parts[(g, t)][:, e, :, 64 * h:64 * (h + 1), :],
+                nc.vector.tensor_tensor(out=parts[(g, t)][:, e, :, 64 * h:64 * (h + 1), :],
                                         in0=w2[:, 0, e], in1=w2[:, 1, e], op=ALU.add)
 
         wt_t = {}
@@ -121,10 +126,17 @@ def tile_primary_capsule_t_kernel(tc, X, weight, out):
         def weight_transposes(g, t, d):
             wt = banks.tile([P, 4, P], F32, name="wt", tag="bank")
             wt_t[(g, t, d)] = wt
+            if (g, t) == SUMMED:
+                for s in range(4):
+                    for e in range(2):
+                        nc.tensor.matmul(out=wt[:, s, :], lhsT=parts[(g, t)][:, e, s, :, d], rhs=ident_f[:],
+                                         start=(e == 0), stop=(e == 1), is_transpose=True)
+                return
+            wv = w_raw[t][:, 2 * g * UNIT:2 * (g + 1) * UNIT].rearrange("i (p s k d) -> i p s k d", s=4, k=K, d=D)
             for s in range(4):
-                for e in range(2):
-                    nc.tensor.matmul(out=wt[:, s, :], lhsT=parts[(g, t)][:, e, s, :, d], rhs=ident_f[:],
-                                     start=(e == 0), stop=(e == 1), is_transpose=True)
+                for k in range(K):
+                    nc.tensor.matmul(out=wt[:, s, :], lhsT=wv[:, :, s, k, d], rhs=ident_b[:],
+                                     start=(k == 0), stop=(k == K - 1))
 
         def weight_copy(g, t, d):
             dst = gw[:, g, d, t * P:(t + 1) * P, :]

@@ -29,8 +29,8 @@ def tile_primary_capsule_t_kernel(tc, X, weight, out):
     Ov = out.rearrange("(m e p) i d -> m p e (i d)", e=2, p=P)
     with ExitStack() as ctx:
         const = ctx.enter_context(tc.tile_pool(name="const", bufs=1))
-        xin = ctx.enter_context(tc.tile_pool(name="xin", bufs=XBUFS))
-        wtmp = ctx.enter_context(tc.tile_pool(name="wtmp", bufs=4))
+        xin = ctx.enter_context(tc.tile_pool(name="xin", bufs=8))
+        wtmp = ctx.enter_context(tc.tile_pool(name="wtmp", bufs=1))
         grp = ctx.enter_context(tc.tile_pool(name="grp", bufs=3))
         xqp = ctx.enter_context(tc.tile_pool(name="xqp", bufs=25))
         ep = ctx.enter_context(tc.tile_pool(name="ep", bufs=4))
@@ -85,7 +85,7 @@ def tile_primary_capsule_t_kernel(tc, X, weight, out):
                 dst = gx_t[n][:, :, g]
                 src = xt_t[n][g][:].rearrange("p t b -> p (t b)").bitcast(BF16).rearrange(
                     "p (t b d) -> p d b t", t=4, d=D)
-                if g == 0 or n % 4 == 0:
+                if g == 0 or n % 3 == 0:
                     nc.scalar.copy(out=dst, in_=src)
                 else:
                     nc.vector.tensor_copy(out=dst, in_=src)
@@ -110,8 +110,6 @@ def tile_primary_capsule_t_kernel(tc, X, weight, out):
             nc.sync.dma_start(out=w_raw[t][:, e0:e0 + UNIT], in_=Wv[t][:, e0:e0 + UNIT])
 
         def weight_add(g, t, h):
-            if (g, t) != SUMMED:
-                return
             e0 = (2 * g + h) * UNIT
             w2 = w_raw[t][:, e0:e0 + UNIT].rearrange("i (p s a e d) -> i a e s p d", s=4, a=2, e=2, d=D)
             if h == 0:
@@ -119,7 +117,7 @@ def tile_primary_capsule_t_kernel(tc, X, weight, out):
                 parts[(g, t)] = part
             for e in range(2):
                 nc.vector.tensor_tensor(out=parts[(g, t)][:, e, :, 64 * h:64 * (h + 1), :],
-                                        in0=w2[:, 0, e], in1=w2[:, 1, e], op=ALU.add)
+                                    in0=w2[:, 0, e], in1=w2[:, 1, e], op=ALU.add)
 
         wt_t = {}
 
@@ -216,10 +214,11 @@ def tile_primary_capsule_t_kernel(tc, X, weight, out):
                     nc.sync.dma_start(out=Ov[m], in_=o_t[m][:].rearrange("p e i d -> p e (i d)"))
 
         order = [(g, t) for g in range(2) for t in range(2)]
-        loads = []
+        loads = [(load, (n,)) for n in range(2)]
         for u in range(8):
-            loads += [(load, (2 * u,)), (load, (2 * u + 1,)), (weight_load, order[u // 2] + (u % 2,))]
-        loads += [(load, (n,)) for n in range(16, HEAD + XBUFS)]
+            loads += [(weight_load, order[u // 2] + (u % 2,))]
+            loads += [(load, (n,)) for n in range(2 + u * 2 // 1, 2 + (u + 1) * 2 // 1)]
+        loads += [(load, (n,)) for n in range(2 + 8 * 2 // 1, HEAD + 7)]
         done_loads = [0]
 
         def issue_loads(n):
@@ -228,19 +227,20 @@ def tile_primary_capsule_t_kernel(tc, X, weight, out):
                 if what is load and args[0] > n + XBUFS - 1:
                     break
                 what(*args)
-                if what is weight_load:
-                    weight_add(*args)
                 done_loads[0] += 1
 
         with tc.manual_schedule(engines={mybir.EngineType.PE}):
             issue_loads(0)
             transposes(0)
             for n in range(HEAD):
-                m, d = divmod(n - 8, 4)
+                m, d = divmod(n - 7, 4)
                 weights_now = 0 <= m < 4 and d < D
                 if weights_now:
                     weight_transposes(*order[m], d)
                 transposes(n + 1)
+                if n == 6 + 4 * order.index(SUMMED):
+                    weight_add(*SUMMED, 0)
+                    weight_add(*SUMMED, 1)
                 copy(n, 0)
                 copy(n, 1)
                 if weights_now:
@@ -251,15 +251,15 @@ def tile_primary_capsule_t_kernel(tc, X, weight, out):
                 issue_loads(n + 1)
             for i in range(-1, NT + 4):
                 ready = HEAD + (i + 1) * (NT + 2 - HEAD) // (NT - 1)
-                transposes(ready + 1)
                 mx(i + 1)
                 rnorm(i - 2)
                 inverse(i - 2)
                 factor(i - 3)
                 add_squares(i - 1)
                 final(i - 3)
-                load(ready + XBUFS - 1)
+                load(ready + 7)
                 quant(ready - 1)
+                transposes(ready)
                 copy(ready, 0)
                 copy(ready, 1)
                 squares(i)

@@ -18,7 +18,7 @@ NT = B // P
 EPS = 1e-8
 TINY = 1e-26
 XBUFS = 8
-SUMMED = (0, 1)
+SUMMED = (1, 0)
 HEAD = 22
 
 
@@ -63,7 +63,11 @@ def tile_primary_capsule_t_kernel(tc, X, weight, out):
         def load(n):
             if 0 <= n < NT and once(("load", n)):
                 x_sb = xin.tile([P, J * D], BF16, name="x_sb")
-                nc.sync.dma_start(out=x_sb[:], in_=Xz[n])
+                if n == 0:
+                    for g in range(2):
+                        nc.sync.dma_start(out=x_sb[:, 1024 * g:1024 * (g + 1)], in_=Xz[n][:, 1024 * g:1024 * (g + 1)])
+                else:
+                    nc.sync.dma_start(out=x_sb[:], in_=Xz[n])
                 x_t[n] = x_sb
 
         def transposes(n):
@@ -85,7 +89,7 @@ def tile_primary_capsule_t_kernel(tc, X, weight, out):
                 dst = gx_t[n][:, :, g]
                 src = xt_t[n][g][:].rearrange("p t b -> p (t b)").bitcast(BF16).rearrange(
                     "p (t b d) -> p d b t", t=4, d=D)
-                if g == 0 or n % 3 == 0:
+                if g == 0 or n % 3 == 2:
                     nc.scalar.copy(out=dst, in_=src)
                 else:
                     nc.vector.tensor_copy(out=dst, in_=src)
@@ -210,7 +214,9 @@ def tile_primary_capsule_t_kernel(tc, X, weight, out):
                     o_t[m] = o_new
                 nc.vector.tensor_tensor(out=o_t[m][:, e], in0=acc_t[n][:].rearrange("p d i -> p i d"),
                                         in1=e_t[n]["f"][:].unsqueeze(2).to_broadcast([P, I, D]), op=ALU.mult)
-                if e == 1:
+                if n >= NT - 2:
+                    nc.sync.dma_start(out=Ov[m][:, e], in_=o_t[m][:, e].rearrange("p i d -> p (i d)"))
+                elif e == 1:
                     nc.sync.dma_start(out=Ov[m], in_=o_t[m][:].rearrange("p e i d -> p e (i d)"))
 
         order = [(g, t) for g in range(2) for t in range(2)]
@@ -250,7 +256,7 @@ def tile_primary_capsule_t_kernel(tc, X, weight, out):
                 quant(n - 1)
                 issue_loads(n + 1)
             for i in range(-1, NT + 4):
-                ready = HEAD + (i + 1) * (NT + 2 - HEAD) // (NT - 1)
+                ready = HEAD + (i + 1) * (NT - HEAD) // (NT - 2)
                 mx(i + 1)
                 rnorm(i - 2)
                 inverse(i - 2)

@@ -19,7 +19,9 @@ EPS = 1e-8
 TINY = 1e-26
 XBUFS = 8
 SUMMED = (1, 0)
-HEAD = 22
+FIRST = 6
+HEAD = 24
+GROUPS = [(2 * m, 2 * m + 1) for m in range(NT // 2 - 1)] + [(NT - 2,), (NT - 1,)]
 
 
 def tile_primary_capsule_t_kernel(tc, X, weight, out):
@@ -31,8 +33,8 @@ def tile_primary_capsule_t_kernel(tc, X, weight, out):
         const = ctx.enter_context(tc.tile_pool(name="const", bufs=1))
         xin = ctx.enter_context(tc.tile_pool(name="xin", bufs=8))
         wtmp = ctx.enter_context(tc.tile_pool(name="wtmp", bufs=1))
-        grp = ctx.enter_context(tc.tile_pool(name="grp", bufs=3))
-        xqp = ctx.enter_context(tc.tile_pool(name="xqp", bufs=25))
+        grp = ctx.enter_context(tc.tile_pool(name="grp", bufs=4))
+        xqp = ctx.enter_context(tc.tile_pool(name="xqp", bufs=27))
         ep = ctx.enter_context(tc.tile_pool(name="ep", bufs=4))
         outp = ctx.enter_context(tc.tile_pool(name="outp", bufs=3))
         banks = ctx.enter_context(tc.psum_pool(name="banks", bufs=8))
@@ -89,7 +91,7 @@ def tile_primary_capsule_t_kernel(tc, X, weight, out):
                 dst = gx_t[n][:, :, g]
                 src = xt_t[n][g][:].rearrange("p t b -> p (t b)").bitcast(BF16).rearrange(
                     "p (t b d) -> p d b t", t=4, d=D)
-                if g == 0 or n % 3 == 2:
+                if g == 0 or n % 3 == 1:
                     nc.scalar.copy(out=dst, in_=src)
                 else:
                     nc.vector.tensor_copy(out=dst, in_=src)
@@ -153,78 +155,81 @@ def tile_primary_capsule_t_kernel(tc, X, weight, out):
                                   scales=wsc[:, g * 2 * I:(g + 1) * 2 * I],
                                   in_=gw[:, g].rearrange("p d i s -> p (d i s)"))
 
-        def mx(n):
-            if 0 <= n < NT:
-                xq, xs = xq_t[n]
-                acc = banks.tile([P, D, I], F32, name="acc", tag="bank")
-                for d in range(D):
-                    for g in range(2):
-                        cx = (2 * d + g) * P
-                        cw = (2 * g + d) * I
-                        nc.tensor.matmul_mx(out=acc[:, d, :],
-                                            lhsT=xq[:, cx:cx + P].bitcast(FP8X4),
-                                            lhsT_scale=xs[:, cx:cx + P],
-                                            rhs=wq[:, cw:cw + I].bitcast(FP8X4),
-                                            rhs_scale=wsc[:, cw:cw + I],
-                                            start=(g == 0), stop=(g == 1))
-                acc_t[n] = acc
+        def mx(m, again=0):
+            if 0 <= m < len(GROUPS):
+                for n in GROUPS[m]:
+                    xq, xs = xq_t[n]
+                    acc = banks.tile([P, D, I], F32, name="acc", tag="bank")
+                    for d in range(D):
+                        for g in range(2):
+                            cx = (2 * d + g) * P
+                            cw = (2 * g + d) * I
+                            nc.tensor.matmul_mx(out=acc[:, d, :],
+                                                lhsT=xq[:, cx:cx + P].bitcast(FP8X4),
+                                                lhsT_scale=xs[:, cx:cx + P],
+                                                rhs=wq[:, cw:cw + I].bitcast(FP8X4),
+                                                rhs_scale=wsc[:, cw:cw + I],
+                                                start=(g == 0), stop=(g == 1))
+                    acc_t[(n, again)] = acc
 
-        def squares(n):
-            if 0 <= n < NT:
-                sq = ep.tile([P, D, I], F32, name="sq")
-                nc.scalar.activation(out=sq[:], in_=acc_t[n][:], func=ACT.Square)
-                e_t[n] = {"sq": sq}
+        def squares(m):
+            if 0 <= m < len(GROUPS):
+                sq = ep.tile([P, len(GROUPS[m]), D, I], F32, name="sq")
+                for e, n in enumerate(GROUPS[m]):
+                    nc.scalar.activation(out=sq[:, e], in_=acc_t[(n, 0)][:], func=ACT.Square)
+                e_t[m] = {"sq": sq}
 
-        def add_squares(n):
-            if 0 <= n < NT:
-                sq = e_t[n]["sq"]
-                n2 = ep.tile([P, I], F32, name="n2")
-                nc.vector.tensor_tensor(out=n2[:], in0=sq[:, 0, :], in1=sq[:, 1, :], op=ALU.add)
-                e_t[n]["n2"] = n2
+        def add_squares(m):
+            if 0 <= m < len(GROUPS):
+                sq = e_t[m]["sq"]
+                n2 = ep.tile([P, len(GROUPS[m]), I], F32, name="n2")
+                nc.vector.tensor_tensor(out=n2[:], in0=sq[:, :, 0, :], in1=sq[:, :, 1, :], op=ALU.add)
+                e_t[m]["n2"] = n2
 
-        def rnorm(n):
-            if 0 <= n < NT:
-                r = ep.tile([P, I], F32, name="r")
-                nc.scalar.activation(out=r[:], in_=e_t[n]["n2"][:], func=ACT.Abs_reciprocal_sqrt,
+        def rnorm(m):
+            if 0 <= m < len(GROUPS):
+                r = ep.tile([P, len(GROUPS[m]), I], F32, name="r")
+                nc.scalar.activation(out=r[:], in_=e_t[m]["n2"][:], func=ACT.Abs_reciprocal_sqrt,
                                      bias=TINY, scale=1.0)
-                e_t[n]["r"] = r
+                e_t[m]["r"] = r
 
-        def inverse(n):
-            if 0 <= n < NT:
-                r = e_t[n]["r"]
-                w = ep.tile([P, I], F32, name="w")
-                nc.vector.scalar_tensor_tensor(out=w[:], in0=r[:], scalar=1.0 / EPS, in1=r[:],
+        def inverse(m):
+            if 0 <= m < len(GROUPS):
+                r = e_t[m]["r"]
+                w = e_t[m]["sq"][:, :, 0, :]
+                nc.vector.scalar_tensor_tensor(out=w, in0=r[:], scalar=1.0 / EPS, in1=r[:],
                                                op0=ALU.add, op1=ALU.mult)
-                nc.vector.scalar_tensor_tensor(out=w[:], in0=e_t[n]["n2"][:], scalar=1.0, in1=w[:],
+                nc.vector.scalar_tensor_tensor(out=w, in0=e_t[m]["n2"][:], scalar=1.0, in1=w,
                                                op0=ALU.add, op1=ALU.mult)
-                e_t[n]["w"] = w
+                e_t[m]["w"] = w
 
-        def factor(n):
-            if 0 <= n < NT:
-                f = ep.tile([P, I], F32, name="f")
-                nc.scalar.activation(out=f[:], in_=e_t[n]["w"][:], func=ACT.Square, scale=EPS)
+        def factor(m):
+            if 0 <= m < len(GROUPS):
+                f = e_t[m]["r"]
+                nc.scalar.activation(out=f[:], in_=e_t[m]["w"], func=ACT.Square, scale=EPS)
                 nc.scalar.activation(out=f[:], in_=f[:], func=ACT.Abs_reciprocal_sqrt)
-                e_t[n]["f"] = f
+                e_t[m]["f"] = f
 
-        def final(n):
-            if 0 <= n < NT:
-                m, e = divmod(n, 2)
-                if e == 0:
-                    o_new = outp.tile([P, 2, I, D], F32, name="o_sb")
-                    o_t[m] = o_new
-                nc.vector.tensor_tensor(out=o_t[m][:, e], in0=acc_t[n][:].rearrange("p d i -> p i d"),
-                                        in1=e_t[n]["f"][:].unsqueeze(2).to_broadcast([P, I, D]), op=ALU.mult)
-                if n >= NT - 2:
-                    nc.sync.dma_start(out=Ov[m][:, e], in_=o_t[m][:, e].rearrange("p i d -> p (i d)"))
-                elif e == 1:
-                    nc.sync.dma_start(out=Ov[m], in_=o_t[m][:].rearrange("p e i d -> p e (i d)"))
+        def final(m):
+            if 0 <= m < len(GROUPS):
+                for e, n in enumerate(GROUPS[m]):
+                    if n % 2 == 0:
+                        o_new = outp.tile([P, 2, I, D], F32, name="o_sb")
+                        o_t[n // 2] = o_new
+                    o_sb = o_t[n // 2]
+                    nc.vector.tensor_tensor(out=o_sb[:, n % 2], in0=acc_t[(n, 1)][:].rearrange("p d i -> p i d"),
+                                            in1=e_t[m]["f"][:, e].unsqueeze(2).to_broadcast([P, I, D]), op=ALU.mult)
+                    if n >= NT - 2:
+                        nc.sync.dma_start(out=Ov[n // 2][:, n % 2], in_=o_sb[:, n % 2].rearrange("p i d -> p (i d)"))
+                    elif n % 2 == 1:
+                        nc.sync.dma_start(out=Ov[n // 2], in_=o_sb[:].rearrange("p e i d -> p e (i d)"))
 
         order = [(g, t) for g in range(2) for t in range(2)]
-        loads = [(load, (n,)) for n in range(2)]
+        loads = [(load, (n,)) for n in range(FIRST)]
         for u in range(8):
             loads += [(weight_load, order[u // 2] + (u % 2,))]
-            loads += [(load, (n,)) for n in range(2 + u * 2 // 1, 2 + (u + 1) * 2 // 1)]
-        loads += [(load, (n,)) for n in range(2 + 8 * 2 // 1, HEAD + 7)]
+            loads += [(load, (n,)) for n in range(FIRST + 2 * u, FIRST + 2 * u + 2)]
+        loads += [(load, (n,)) for n in range(FIRST + 16, HEAD + 7)]
         done_loads = [0]
 
         def issue_loads(n):
@@ -239,7 +244,7 @@ def tile_primary_capsule_t_kernel(tc, X, weight, out):
             issue_loads(0)
             transposes(0)
             for n in range(HEAD):
-                m, d = divmod(n - 7, 4)
+                m, d = divmod(n - 8, 4)
                 weights_now = 0 <= m < 4 and d < D
                 if weights_now:
                     weight_transposes(*order[m], d)
@@ -255,17 +260,19 @@ def tile_primary_capsule_t_kernel(tc, X, weight, out):
                         weight_quant(m // 2)
                 quant(n - 1)
                 issue_loads(n + 1)
-            for i in range(-1, NT + 4):
-                ready = HEAD + (i + 1) * (NT - HEAD) // (NT - 2)
-                mx(i + 1)
-                rnorm(i - 2)
-                inverse(i - 2)
-                factor(i - 3)
-                add_squares(i - 1)
-                final(i - 3)
-                load(ready + 7)
-                quant(ready - 1)
-                transposes(ready)
-                copy(ready, 0)
-                copy(ready, 1)
-                squares(i)
+            for m in range(-1, len(GROUPS) + 4):
+                mx(m - 3, 1)
+                mx(m + 1)
+                rnorm(m - 1)
+                inverse(m - 2)
+                final(m - 3)
+                factor(m - 2)
+                for ready in range(HEAD + (m + 1) * (NT - HEAD) // 14, HEAD + (m + 2) * (NT - HEAD) // 14):
+                    load(ready + 7)
+                    quant(ready - 1)
+                    transposes(ready)
+                    copy(ready, 0)
+                    copy(ready, 1)
+                quant(HEAD + (m + 2) * (NT - HEAD) // 14 - 1)
+                squares(m)
+                add_squares(m)

from contextlib import ExitStack

import concourse.mybir as mybir
from concourse.masks import make_identity

F32 = mybir.dt.float32
BF16 = mybir.dt.bfloat16
U32 = mybir.dt.uint32
U8 = mybir.dt.uint8
FP8X4 = mybir.dt.float8_e4m3fn_x4
ACT = mybir.ActivationFunctionType
ALU = mybir.AluOpType

B, I, J, K, D = 4096, 256, 1024, 4, 2
P = 128
FLOPS = 2 * B * I * J * D
NT = B // P
EPS = 1e-8
TINY = 1e-26
XBUFS = 8
SUMMED = (1, 0)
FIRST = 6
HEAD = 24
GROUPS = [(2 * m, 2 * m + 1) for m in range(NT // 2 - 1)] + [(NT - 2,), (NT - 1,)]


def tile_primary_capsule_t_kernel(tc, X, weight, out):
    nc = tc.nc
    Xz = X.rearrange("(n q) j d -> n q (j d)", q=P)
    Wv = weight.rearrange("(t p) j k d -> t p (j k d)", p=P)
    Ov = out.rearrange("(m e p) i d -> m p e (i d)", e=2, p=P)
    with ExitStack() as ctx:
        const = ctx.enter_context(tc.tile_pool(name="const", bufs=1))
        xin = ctx.enter_context(tc.tile_pool(name="xin", bufs=8))
        wtmp = ctx.enter_context(tc.tile_pool(name="wtmp", bufs=1))
        grp = ctx.enter_context(tc.tile_pool(name="grp", bufs=4))
        xqp = ctx.enter_context(tc.tile_pool(name="xqp", bufs=27))
        ep = ctx.enter_context(tc.tile_pool(name="ep", bufs=4))
        outp = ctx.enter_context(tc.tile_pool(name="outp", bufs=3))
        banks = ctx.enter_context(tc.psum_pool(name="banks", bufs=8))

        warm = const.tile([P, 1], F32, name="warm")
        nc.vector.memset(warm[:], 1.0)
        nc.scalar.activation(out=warm[:], in_=warm[:], func=ACT.Abs_reciprocal_sqrt)
        ident_b = const.tile([P, P], BF16, name="ident_b")
        make_identity(nc, ident_b[:])
        ident_f = const.tile([P, P], F32, name="ident_f")
        make_identity(nc, ident_f[:])

        x_t = {}
        xt_t = {}
        gx_t = {}
        xq_t = {}
        acc_t = {}
        e_t = {}
        o_t = {}
        done = set()

        def once(key):
            if key in done:
                return False
            done.add(key)
            return True

        def load(n):
            if 0 <= n < NT and once(("load", n)):
                x_sb = xin.tile([P, J * D], BF16, name="x_sb")
                if n == 0:
                    for g in range(2):
                        nc.sync.dma_start(out=x_sb[:, 1024 * g:1024 * (g + 1)], in_=Xz[n][:, 1024 * g:1024 * (g + 1)])
                else:
                    nc.sync.dma_start(out=x_sb[:], in_=Xz[n])
                x_t[n] = x_sb

        def transposes(n):
            if 0 <= n < NT and once(("T", n)):
                xts = []
                words = x_t[n][:].bitcast(F32)
                for g in range(2):
                    xt = banks.tile([P, 4, P], F32, name="xt", tag="bank")
                    for t in range(4):
                        nc.tensor.transpose(xt[:, t, :], words[:, 512 * g + t:512 * (g + 1):4], ident_f[:])
                    xts.append(xt)
                xt_t[n] = xts

        def copy(n, g):
            if 0 <= n < NT and once(("c", n, g)):
                if g == 0:
                    gx_new = grp.tile([P, D, 2, P, 4], BF16, name="gx", align_bytes=64)
                    gx_t[n] = gx_new
                dst = gx_t[n][:, :, g]
                src = xt_t[n][g][:].rearrange("p t b -> p (t b)").bitcast(BF16).rearrange(
                    "p (t b d) -> p d b t", t=4, d=D)
                if g == 0 or n % 3 == 1:
                    nc.scalar.copy(out=dst, in_=src)
                else:
                    nc.vector.tensor_copy(out=dst, in_=src)

        def quant(n):
            if 0 <= n < NT and once(("Q", n)):
                xq = xqp.tile([P, 4 * P], U32, name="xq", align_bytes=64)
                xs = xqp.tile([P, 4 * P], U8, name="xs", align_bytes=64)
                nc.vector.quantize_mx(out=xq[:].bitcast(FP8X4), scales=xs[:],
                                      in_=gx_t[n][:].rearrange("p d g b s -> p (d g b s)"))
                xq_t[n] = (xq, xs)

        UNIT = 256 * K * D
        w_raw = [const.tile([P, J * K * D], BF16, name="w_raw%d" % t) for t in range(2)]
        gw = const.tile([P, 2, D, I, 4], BF16, name="gw", align_bytes=64)
        wq = const.tile([P, 4 * I], U32, name="wq", align_bytes=64)
        wsc = const.tile([P, 4 * I], U8, name="wsc", align_bytes=64)
        parts = {}

        def weight_load(g, t, h):
            e0 = (2 * g + h) * UNIT
            nc.sync.dma_start(out=w_raw[t][:, e0:e0 + UNIT], in_=Wv[t][:, e0:e0 + UNIT])

        def weight_add(g, t, h):
            e0 = (2 * g + h) * UNIT
            w2 = w_raw[t][:, e0:e0 + UNIT].rearrange("i (p s a e d) -> i a e s p d", s=4, a=2, e=2, d=D)
            if h == 0:
                part = wtmp.tile([P, 2, 4, P, D], F32, name="part")
                parts[(g, t)] = part
            for e in range(2):
                nc.vector.tensor_tensor(out=parts[(g, t)][:, e, :, 64 * h:64 * (h + 1), :],
                                    in0=w2[:, 0, e], in1=w2[:, 1, e], op=ALU.add)

        wt_t = {}

        def weight_transposes(g, t, d):
            wt = banks.tile([P, 4, P], F32, name="wt", tag="bank")
            wt_t[(g, t, d)] = wt
            if (g, t) == SUMMED:
                for s in range(4):
                    for e in range(2):
                        nc.tensor.matmul(out=wt[:, s, :], lhsT=parts[(g, t)][:, e, s, :, d], rhs=ident_f[:],
                                         start=(e == 0), stop=(e == 1), is_transpose=True)
                return
            wv = w_raw[t][:, 2 * g * UNIT:2 * (g + 1) * UNIT].rearrange("i (p s k d) -> i p s k d", s=4, k=K, d=D)
            for s in range(4):
                for k in range(K):
                    nc.tensor.matmul(out=wt[:, s, :], lhsT=wv[:, :, s, k, d], rhs=ident_b[:],
                                     start=(k == 0), stop=(k == K - 1))

        def weight_copy(g, t, d):
            dst = gw[:, g, d, t * P:(t + 1) * P, :]
            src = wt_t[(g, t, d)][:].rearrange("p s i -> p i s")
            if d == 0:
                nc.scalar.copy(out=dst, in_=src)
            else:
                nc.vector.tensor_copy(out=dst, in_=src)

        def weight_quant(g):
            nc.vector.quantize_mx(out=wq[:, g * 2 * I:(g + 1) * 2 * I].bitcast(FP8X4),
                                  scales=wsc[:, g * 2 * I:(g + 1) * 2 * I],
                                  in_=gw[:, g].rearrange("p d i s -> p (d i s)"))

        def mx(m, again=0):
            if 0 <= m < len(GROUPS):
                for n in GROUPS[m]:
                    xq, xs = xq_t[n]
                    acc = banks.tile([P, D, I], F32, name="acc", tag="bank")
                    for d in range(D):
                        for g in range(2):
                            cx = (2 * d + g) * P
                            cw = (2 * g + d) * I
                            nc.tensor.matmul_mx(out=acc[:, d, :],
                                                lhsT=xq[:, cx:cx + P].bitcast(FP8X4),
                                                lhsT_scale=xs[:, cx:cx + P],
                                                rhs=wq[:, cw:cw + I].bitcast(FP8X4),
                                                rhs_scale=wsc[:, cw:cw + I],
                                                start=(g == 0), stop=(g == 1))
                    acc_t[(n, again)] = acc

        def squares(m):
            if 0 <= m < len(GROUPS):
                sq = ep.tile([P, len(GROUPS[m]), D, I], F32, name="sq")
                for e, n in enumerate(GROUPS[m]):
                    nc.scalar.activation(out=sq[:, e], in_=acc_t[(n, 0)][:], func=ACT.Square)
                e_t[m] = {"sq": sq}

        def add_squares(m):
            if 0 <= m < len(GROUPS):
                sq = e_t[m]["sq"]
                n2 = ep.tile([P, len(GROUPS[m]), I], F32, name="n2")
                nc.vector.tensor_tensor(out=n2[:], in0=sq[:, :, 0, :], in1=sq[:, :, 1, :], op=ALU.add)
                e_t[m]["n2"] = n2

        def rnorm(m):
            if 0 <= m < len(GROUPS):
                r = ep.tile([P, len(GROUPS[m]), I], F32, name="r")
                nc.scalar.activation(out=r[:], in_=e_t[m]["n2"][:], func=ACT.Abs_reciprocal_sqrt,
                                     bias=TINY, scale=1.0)
                e_t[m]["r"] = r

        def inverse(m):
            if 0 <= m < len(GROUPS):
                r = e_t[m]["r"]
                w = e_t[m]["sq"][:, :, 0, :]
                nc.vector.scalar_tensor_tensor(out=w, in0=r[:], scalar=1.0 / EPS, in1=r[:],
                                               op0=ALU.add, op1=ALU.mult)
                nc.vector.scalar_tensor_tensor(out=w, in0=e_t[m]["n2"][:], scalar=1.0, in1=w,
                                               op0=ALU.add, op1=ALU.mult)
                e_t[m]["w"] = w

        def factor(m):
            if 0 <= m < len(GROUPS):
                f = e_t[m]["r"]
                nc.scalar.activation(out=f[:], in_=e_t[m]["w"], func=ACT.Square, scale=EPS)
                nc.scalar.activation(out=f[:], in_=f[:], func=ACT.Abs_reciprocal_sqrt)
                e_t[m]["f"] = f

        def final(m):
            if 0 <= m < len(GROUPS):
                for e, n in enumerate(GROUPS[m]):
                    if n % 2 == 0:
                        o_new = outp.tile([P, 2, I, D], F32, name="o_sb")
                        o_t[n // 2] = o_new
                    o_sb = o_t[n // 2]
                    nc.vector.tensor_tensor(out=o_sb[:, n % 2], in0=acc_t[(n, 1)][:].rearrange("p d i -> p i d"),
                                            in1=e_t[m]["f"][:, e].unsqueeze(2).to_broadcast([P, I, D]), op=ALU.mult)
                    if n >= NT - 2:
                        nc.sync.dma_start(out=Ov[n // 2][:, n % 2], in_=o_sb[:, n % 2].rearrange("p i d -> p (i d)"))
                    elif n % 2 == 1:
                        nc.sync.dma_start(out=Ov[n // 2], in_=o_sb[:].rearrange("p e i d -> p e (i d)"))

        order = [(g, t) for g in range(2) for t in range(2)]
        loads = [(load, (n,)) for n in range(FIRST)]
        for u in range(8):
            loads += [(weight_load, order[u // 2] + (u % 2,))]
            loads += [(load, (n,)) for n in range(FIRST + 2 * u, FIRST + 2 * u + 2)]
        loads += [(load, (n,)) for n in range(FIRST + 16, HEAD + 7)]
        done_loads = [0]

        def issue_loads(n):
            while done_loads[0] < len(loads):
                what, args = loads[done_loads[0]]
                if what is load and args[0] > n + XBUFS - 1:
                    break
                what(*args)
                done_loads[0] += 1

        with tc.manual_schedule(engines={mybir.EngineType.PE}):
            issue_loads(0)
            transposes(0)
            for n in range(HEAD):
                m, d = divmod(n - 8, 4)
                weights_now = 0 <= m < 4 and d < D
                if weights_now:
                    weight_transposes(*order[m], d)
                transposes(n + 1)
                if n == 6 + 4 * order.index(SUMMED):
                    weight_add(*SUMMED, 0)
                    weight_add(*SUMMED, 1)
                copy(n, 0)
                copy(n, 1)
                if weights_now:
                    weight_copy(*order[m], d)
                    if d == 1 and m % 2 == 1:
                        weight_quant(m // 2)
                quant(n - 1)
                issue_loads(n + 1)
            for m in range(-1, len(GROUPS) + 4):
                mx(m - 3, 1)
                mx(m + 1)
                rnorm(m - 1)
                inverse(m - 2)
                final(m - 3)
                factor(m - 2)
                for ready in range(HEAD + (m + 1) * (NT - HEAD) // 14, HEAD + (m + 2) * (NT - HEAD) // 14):
                    load(ready + 7)
                    quant(ready - 1)
                    transposes(ready)
                    copy(ready, 0)
                    copy(ready, 1)
                quant(HEAD + (m + 2) * (NT - HEAD) // 14 - 1)
                squares(m)
                add_squares(m)
